import numpy as np
import ml_dtypes


def mxq(x, axis, fmt="e4m3"):
    dtype, down = {"e4m3": (ml_dtypes.float8_e4m3fn, 7), "e5m2": (ml_dtypes.float8_e5m2, 14)}[fmt]
    v = np.moveaxis(np.asarray(x, np.float32).astype(ml_dtypes.bfloat16).astype(np.float64), axis, -1)
    blocks = v.reshape(v.shape[:-1] + (-1, 32))
    amax = np.abs(blocks).max(-1, keepdims=True)
    byte = np.maximum(np.where(amax > 0, np.frexp(amax)[1] - 1 + 127, 0) - down, 1)
    scale = np.exp2(byte - 127.0)
    codes = (blocks / scale).astype(np.float32).astype(dtype).astype(np.float64)
    return np.moveaxis((codes * scale).reshape(v.shape), -1, axis)


WIDE = False


def mx_kscale(k):
    if not WIDE:
        return np.ones(k)
    levels = np.array([10, -10, 5, -5, 0])
    a = np.random.permutation(np.resize(levels, k // 512 * 4)).reshape(k // 512, 4)
    idx = np.arange(k)
    return np.exp2(a[idx // 512, idx % 128 // 32])


BF16 = ml_dtypes.bfloat16


def bf(x):
    return np.asarray(x, np.float32).astype(BF16)


def f64(x):
    return np.asarray(x).astype(np.float64)


B, N, F_IN, F_OUT, K = 32, 512, 128, 256, 4


def setup_inputs():
    s = mx_kscale(N)
    r = (s.min() / s)[:, None]
    return {"x": bf(np.random.standard_normal((B, N, F_IN)) * r),
            "L": bf(np.random.standard_normal((N, N)) * 0.7 / np.sqrt(N) * s[None, :] / s[:, None])}


def reference(x, L):
    Lq = mxq(f64(L), 1, "e4m3")
    x1 = Lq @ mxq(f64(x), 1, "e4m3")
    x2 = Lq @ mxq(x1, 1, "e4m3")
    xt2 = 2.0 * x2 - f64(x)
    return x1, x2, xt2

@@ -1,0 +1,157 @@
+from contextlib import ExitStack
+
+import concourse.masks as masks
+import concourse.mybir as mybir
+
+F32 = mybir.dt.float32
+BF16 = mybir.dt.bfloat16
+U32 = mybir.dt.uint32
+U8 = mybir.dt.uint8
+FP8X4 = mybir.dt.float8_e4m3fn_x4
+MULT = mybir.AluOpType.mult
+SUB = mybir.AluOpType.subtract
+
+P = 128
+PACK = 4
+B, N, F = 32, 512, 128
+GB = 4
+NG = B // GB
+W = GB * F
+FLOPS = 2 * 2 * B * N * N * F
+
+
+def tile_gcncheb_pa_t_kernel(tc, x, L, out_0, out_1, out_2):
+    nc = tc.nc
+    with ExitStack() as ctx:
+        keep = ctx.enter_context(tc.tile_pool(name="keep", bufs=1))
+        stage = ctx.enter_context(tc.tile_pool(name="stage", bufs=3))
+        outs = ctx.enter_context(tc.tile_pool(name="outs", bufs=16))
+        psum = ctx.enter_context(tc.psum_pool(name="psum", bufs=8))
+
+        def dram_group(t, g):
+            return t[g * GB:(g + 1) * GB].rearrange("c (p j) f -> p c (j f)", j=PACK)
+
+        l_raw = keep.tile([P, PACK * N], BF16, name="l_raw")
+        nc.sync.dma_start(out=l_raw[:], in_=L.rearrange("(q j) m -> q (j m)", j=PACK))
+        x_raw = []
+        for g in range(NG):
+            xr = keep.tile([P, GB, PACK * F], BF16, name="x_raw%d" % g)
+            nc.sync.dma_start(out=xr[:], in_=dram_group(x, g))
+            x_raw.append(xr)
+
+        ident = keep.tile([P, P], F32, name="ident")
+        masks.make_identity(nc, ident[:])
+
+        l_words = l_raw[:].bitcast(F32).rearrange("q (j w u) -> q j u w", j=PACK, u=2)
+        l_grouped = keep.tile([P, PACK * N], BF16, name="l_grouped", align_bytes=64)
+        l_grouped_w = l_grouped[:].bitcast(F32).rearrange("p (j q u) -> p j q u", j=PACK, u=2)
+        for h in range(2):
+            lt = psum.tile([P, 4, P], F32, tag="bank", name="lt")
+            for jj in range(2):
+                for u in range(2):
+                    nc.tensor.transpose(lt[:, 2 * jj + u, :], l_words[:, 2 * h + jj, u, :], ident[:])
+            nc.scalar.copy(
+                out=l_grouped_w[:, 2 * h:2 * h + 2, :, :],
+                in_=lt[:].rearrange("p (jj u) q -> p jj q u", u=2),
+            )
+        l_codes = keep.tile([P, N], U32, name="l_codes", align_bytes=64)
+        l_scales = keep.tile([P, N], U8, name="l_scales", align_bytes=64)
+
+        def quant_l():
+            nc.vector.quantize_mx(out=l_codes[:].bitcast(FP8X4), scales=l_scales[:], in_=l_grouped[:])
+
+        x_grouped = {}
+        x_codes = {}
+        x_scales = {}
+        y_grouped = {}
+        y_codes = {}
+        y_scales = {}
+        o1 = {}
+        o2 = {}
+
+        def regroup_x(g):
+            t = stage.tile([P, PACK * W], BF16, tag="xg", name="xg", align_bytes=64)
+            nc.vector.tensor_copy(
+                out=t[:].rearrange("p (c f t) -> p c f t", c=GB, t=PACK),
+                in_=x_raw[g][:].rearrange("p c (t f) -> p c f t", t=PACK),
+            )
+            x_grouped[g] = t
+
+        def quant_x(g):
+            x_codes[g] = keep.tile([P, W], U32, name="x_codes%d" % g, align_bytes=64)
+            x_scales[g] = keep.tile([P, W], U8, name="x_scales%d" % g, align_bytes=64)
+            nc.vector.quantize_mx(out=x_codes[g][:].bitcast(FP8X4), scales=x_scales[g][:], in_=x_grouped[g][:])
+
+        def hop(codes, scales, dst, dram):
+            for c in range(GB):
+                bank = psum.tile([P, PACK * F], F32, tag="bank", name="bank")
+                for j in range(PACK):
+                    nc.tensor.matmul_mx(
+                        out=bank[:, j * F:(j + 1) * F],
+                        lhsT=l_codes[:, j * P:(j + 1) * P].bitcast(FP8X4),
+                        lhsT_scale=l_scales[:, j * P:(j + 1) * P],
+                        rhs=codes[:, c * F:(c + 1) * F].bitcast(FP8X4),
+                        rhs_scale=scales[:, c * F:(c + 1) * F],
+                        start=True,
+                        stop=True,
+                    )
+                nc.scalar.copy(out=dst[:, c, :], in_=bank[:])
+            nc.sync.dma_start(out=dram, in_=dst[:])
+
+        def hop1(g):
+            o1[g] = outs.tile([P, GB, PACK * F], F32, tag="o", name="o1")
+            hop(x_codes[g], x_scales[g], o1[g], dram_group(out_0, g))
+
+        def regroup_y(g):
+            t = stage.tile([P, PACK * W], BF16, tag="yg", name="yg", align_bytes=64)
+            nc.vector.tensor_copy(
+                out=t[:].rearrange("p (c f t) -> p c f t", c=GB, t=PACK),
+                in_=o1[g][:].rearrange("p c (t f) -> p c f t", t=PACK),
+            )
+            y_grouped[g] = t
+
+        def quant_y(g):
+            y_codes[g] = stage.tile([P, W], U32, tag="yc", name="yc", align_bytes=64)
+            y_scales[g] = stage.tile([P, W], U8, tag="ys", name="ys", align_bytes=64)
+            nc.vector.quantize_mx(out=y_codes[g][:].bitcast(FP8X4), scales=y_scales[g][:], in_=y_grouped[g][:])
+
+        def hop2(g):
+            o2[g] = outs.tile([P, GB, PACK * F], F32, tag="o", name="o2")
+            hop(y_codes[g], y_scales[g], o2[g], dram_group(out_1, g))
+
+        def recurrence(g):
+            o3 = outs.tile([P, GB, PACK * F], F32, tag="o", name="o3")
+            nc.vector.scalar_tensor_tensor(
+                out=o3[:].rearrange("p c n -> p (c n)"),
+                in0=o2[g][:].rearrange("p c n -> p (c n)"),
+                scalar=2.0,
+                in1=x_raw[g][:].rearrange("p c n -> p (c n)"),
+                op0=MULT,
+                op1=SUB,
+            )
+            nc.sync.dma_start(out=dram_group(out_2, g), in_=o3[:])
+
+        regroup_x(0)
+        quant_l()
+        regroup_x(1)
+        quant_x(0)
+        quant_x(1)
+        hop1(0)
+        hop1(1)
+        regroup_x(2)
+        regroup_x(3)
+        quant_x(2)
+        quant_x(3)
+        for g in range(NG):
+            regroup_y(g)
+            if g + 4 < NG:
+                regroup_x(g + 4)
+            quant_y(g)
+            if g + 4 < NG:
+                quant_x(g + 4)
+            hop2(g)
+            if g >= 1:
+                recurrence(g - 1)
+            if g + 2 < NG:
+                hop1(g + 2)
+        recurrence(NG - 1)

@@ -27,6 +27,7 @@ def tile_gcncheb_pa_t_kernel(tc, x, L, out_0, out_1, out_2):
         stage = ctx.enter_context(tc.tile_pool(name="stage", bufs=3))
         outs = ctx.enter_context(tc.tile_pool(name="outs", bufs=16))
         psum = ctx.enter_context(tc.psum_pool(name="psum", bufs=8))
+        ctx.enter_context(tc.manual_schedule())
 
         def dram_group(t, g):
             return t[g * GB:(g + 1) * GB].rearrange("c (p j) f -> p c (j f)", j=PACK)
@@ -132,26 +133,23 @@ def tile_gcncheb_pa_t_kernel(tc, x, L, out_0, out_1, out_2):
             nc.sync.dma_start(out=dram_group(out_2, g), in_=o3[:])
 
         regroup_x(0)
-        quant_l()
-        regroup_x(1)
         quant_x(0)
-        quant_x(1)
+        quant_l()
         hop1(0)
-        hop1(1)
-        regroup_x(2)
-        regroup_x(3)
-        quant_x(2)
-        quant_x(3)
+        for g in (1, 2):
+            regroup_x(g)
+            quant_x(g)
+            hop1(g)
         for g in range(NG):
+            a = g + 3
             regroup_y(g)
-            if g + 4 < NG:
-                regroup_x(g + 4)
+            if a < NG:
+                regroup_x(a)
             quant_y(g)
-            if g + 4 < NG:
-                quant_x(g + 4)
             hop2(g)
+            if a < NG:
+                quant_x(a)
+                hop1(a)
             if g >= 1:
                 recurrence(g - 1)
-            if g + 2 < NG:
-                hop1(g + 2)
         recurrence(NG - 1)

@@ -84,19 +84,18 @@ def tile_gcncheb_pa_t_kernel(tc, x, L, out_0, out_1, out_2):
             nc.vector.quantize_mx(out=x_codes[g][:].bitcast(FP8X4), scales=x_scales[g][:], in_=x_grouped[g][:])
 
         def hop(codes, scales, dst, dram):
-            for c in range(GB):
-                bank = psum.tile([P, PACK * F], F32, tag="bank", name="bank")
-                for j in range(PACK):
-                    nc.tensor.matmul_mx(
-                        out=bank[:, j * F:(j + 1) * F],
-                        lhsT=l_codes[:, j * P:(j + 1) * P].bitcast(FP8X4),
-                        lhsT_scale=l_scales[:, j * P:(j + 1) * P],
-                        rhs=codes[:, c * F:(c + 1) * F].bitcast(FP8X4),
-                        rhs_scale=scales[:, c * F:(c + 1) * F],
-                        start=True,
-                        stop=True,
-                    )
-                nc.scalar.copy(out=dst[:, c, :], in_=bank[:])
+            for j in range(PACK):
+                bank = psum.tile([P, GB, F], F32, tag="bank", name="bank")
+                nc.tensor.matmul_mx(
+                    out=bank[:].rearrange("p c f -> p (c f)"),
+                    lhsT=l_codes[:, j * P:(j + 1) * P].bitcast(FP8X4),
+                    lhsT_scale=l_scales[:, j * P:(j + 1) * P],
+                    rhs=codes[:].bitcast(FP8X4),
+                    rhs_scale=scales[:],
+                    start=True,
+                    stop=True,
+                )
+                nc.scalar.copy(out=dst[:, :, j * F:(j + 1) * F], in_=bank[:])
             nc.sync.dma_start(out=dram, in_=dst[:])
 
         def hop1(g):

@@ -8,16 +8,18 @@ BF16 = mybir.dt.bfloat16
 U32 = mybir.dt.uint32
 U8 = mybir.dt.uint8
 FP8X4 = mybir.dt.float8_e4m3fn_x4
-MULT = mybir.AluOpType.mult
-SUB = mybir.AluOpType.subtract
 
 P = 128
 PACK = 4
-B, N, F = 32, 512, 128
-GB = 4
-NG = B // GB
-W = GB * F
-FLOPS = 2 * 2 * B * N * N * F
+PAIRS = 2
+SETS_IN_BANK = 2
+BATCH, NODES, FEATURES = 32, 512, 128
+GROUP = 4
+N_GROUPS = BATCH // GROUP
+COLUMNS = GROUP * FEATURES
+ROW = PACK * FEATURES
+AHEAD = 3
+FLOPS = 2 * 2 * BATCH * NODES * NODES * FEATURES
 
 
 def tile_gcncheb_pa_t_kernel(tc, x, L, out_0, out_1, out_2):
@@ -25,130 +27,128 @@ def tile_gcncheb_pa_t_kernel(tc, x, L, out_0, out_1, out_2):
     with ExitStack() as ctx:
         keep = ctx.enter_context(tc.tile_pool(name="keep", bufs=1))
         stage = ctx.enter_context(tc.tile_pool(name="stage", bufs=3))
-        outs = ctx.enter_context(tc.tile_pool(name="outs", bufs=16))
+        results = ctx.enter_context(tc.tile_pool(name="results", bufs=16))
         psum = ctx.enter_context(tc.psum_pool(name="psum", bufs=8))
         ctx.enter_context(tc.manual_schedule())
 
-        def dram_group(t, g):
-            return t[g * GB:(g + 1) * GB].rearrange("c (p j) f -> p c (j f)", j=PACK)
+        def dram_group(tensor, g):
+            return tensor[g * GROUP:(g + 1) * GROUP].rearrange("c (p t) f -> p c (t f)", t=PACK)
 
-        l_raw = keep.tile([P, PACK * N], BF16, name="l_raw")
+        l_raw = keep.tile([P, PACK * NODES], BF16, name="l_raw")
         nc.sync.dma_start(out=l_raw[:], in_=L.rearrange("(q j) m -> q (j m)", j=PACK))
         x_raw = []
-        for g in range(NG):
-            xr = keep.tile([P, GB, PACK * F], BF16, name="x_raw%d" % g)
-            nc.sync.dma_start(out=xr[:], in_=dram_group(x, g))
-            x_raw.append(xr)
+        for g in range(N_GROUPS):
+            x_raw.append(keep.tile([P, GROUP, ROW], BF16, name="x_raw%d" % g))
+            nc.sync.dma_start(out=x_raw[g][:], in_=dram_group(x, g))
 
-        ident = keep.tile([P, P], F32, name="ident")
-        masks.make_identity(nc, ident[:])
-
-        l_words = l_raw[:].bitcast(F32).rearrange("q (j w u) -> q j u w", j=PACK, u=2)
-        l_grouped = keep.tile([P, PACK * N], BF16, name="l_grouped", align_bytes=64)
-        l_grouped_w = l_grouped[:].bitcast(F32).rearrange("p (j q u) -> p j q u", j=PACK, u=2)
-        for h in range(2):
-            lt = psum.tile([P, 4, P], F32, tag="bank", name="lt")
-            for jj in range(2):
-                for u in range(2):
-                    nc.tensor.transpose(lt[:, 2 * jj + u, :], l_words[:, 2 * h + jj, u, :], ident[:])
+        identity = keep.tile([P, P], F32, name="identity")
+        masks.make_identity(nc, identity[:])
+        l_words = l_raw[:].bitcast(F32).rearrange("q (j p u) -> q j u p", j=PACK, u=PAIRS)
+        l_grouped = keep.tile([P, PACK * NODES], BF16, name="l_grouped", align_bytes=64)
+        l_grouped_words = l_grouped[:].bitcast(F32).rearrange("p (j q u) -> p j q u", j=PACK, u=PAIRS)
+        for first_set in range(0, PACK, SETS_IN_BANK):
+            transposed = psum.tile([P, SETS_IN_BANK * PAIRS, P], F32, tag="bank", name="transposed")
+            for s in range(SETS_IN_BANK):
+                for u in range(PAIRS):
+                    nc.tensor.transpose(transposed[:, PAIRS * s + u, :], l_words[:, first_set + s, u, :], identity[:])
             nc.scalar.copy(
-                out=l_grouped_w[:, 2 * h:2 * h + 2, :, :],
-                in_=lt[:].rearrange("p (jj u) q -> p jj q u", u=2),
+                out=l_grouped_words[:, first_set:first_set + SETS_IN_BANK, :, :],
+                in_=transposed[:].rearrange("p (s u) q -> p s q u", u=PAIRS),
             )
-        l_codes = keep.tile([P, N], U32, name="l_codes", align_bytes=64)
-        l_scales = keep.tile([P, N], U8, name="l_scales", align_bytes=64)
+        l_codes = keep.tile([P, NODES], U32, name="l_codes", align_bytes=64)
+        l_scales = keep.tile([P, NODES], U8, name="l_scales", align_bytes=64)
 
-        def quant_l():
+        def quantise_l():
             nc.vector.quantize_mx(out=l_codes[:].bitcast(FP8X4), scales=l_scales[:], in_=l_grouped[:])
 
-        x_grouped = {}
-        x_codes = {}
-        x_scales = {}
-        y_grouped = {}
-        y_codes = {}
-        y_scales = {}
-        o1 = {}
-        o2 = {}
+        grouped = {}
+        codes = {}
+        scales = {}
+        x1_result = {}
+        x2_result = {}
 
-        def regroup_x(g):
-            t = stage.tile([P, PACK * W], BF16, tag="xg", name="xg", align_bytes=64)
+        def regroup(name, g, source):
+            label = name + "_grouped"
+            grouped[name, g] = stage.tile([P, PACK * COLUMNS], BF16, tag=label, name=label, align_bytes=64)
             nc.vector.tensor_copy(
-                out=t[:].rearrange("p (c f t) -> p c f t", c=GB, t=PACK),
-                in_=x_raw[g][:].rearrange("p c (t f) -> p c f t", t=PACK),
+                out=grouped[name, g][:].rearrange("p (c f t) -> p c f t", c=GROUP, t=PACK),
+                in_=source[:].rearrange("p c (t f) -> p c f t", t=PACK),
             )
-            x_grouped[g] = t
 
-        def quant_x(g):
-            x_codes[g] = keep.tile([P, W], U32, name="x_codes%d" % g, align_bytes=64)
-            x_scales[g] = keep.tile([P, W], U8, name="x_scales%d" % g, align_bytes=64)
-            nc.vector.quantize_mx(out=x_codes[g][:].bitcast(FP8X4), scales=x_scales[g][:], in_=x_grouped[g][:])
+        def quantise(name, g, pool, suffix):
+            label = name + "_codes" + suffix
+            codes[name, g] = pool.tile([P, COLUMNS], U32, tag=label, name=label, align_bytes=64)
+            label = name + "_scales" + suffix
+            scales[name, g] = pool.tile([P, COLUMNS], U8, tag=label, name=label, align_bytes=64)
+            nc.vector.quantize_mx(
+                out=codes[name, g][:].bitcast(FP8X4), scales=scales[name, g][:], in_=grouped[name, g][:]
+            )
 
-        def hop(codes, scales, dst, dram):
+        def hop(name, g, destination):
+            result = results.tile([P, GROUP, ROW], F32, tag="result", name="result")
             for j in range(PACK):
-                bank = psum.tile([P, GB, F], F32, tag="bank", name="bank")
+                bank = psum.tile([P, GROUP, FEATURES], F32, tag="bank", name="bank")
                 nc.tensor.matmul_mx(
                     out=bank[:].rearrange("p c f -> p (c f)"),
                     lhsT=l_codes[:, j * P:(j + 1) * P].bitcast(FP8X4),
                     lhsT_scale=l_scales[:, j * P:(j + 1) * P],
-                    rhs=codes[:].bitcast(FP8X4),
-                    rhs_scale=scales[:],
+                    rhs=codes[name, g][:].bitcast(FP8X4),
+                    rhs_scale=scales[name, g][:],
                     start=True,
                     stop=True,
                 )
-                nc.scalar.copy(out=dst[:, :, j * F:(j + 1) * F], in_=bank[:])
-            nc.sync.dma_start(out=dram, in_=dst[:])
+                nc.scalar.copy(out=result[:, :, j * FEATURES:(j + 1) * FEATURES], in_=bank[:])
+            nc.sync.dma_start(out=dram_group(destination, g), in_=result[:])
+            return result
 
-        def hop1(g):
-            o1[g] = outs.tile([P, GB, PACK * F], F32, tag="o", name="o1")
-            hop(x_codes[g], x_scales[g], o1[g], dram_group(out_0, g))
+        def regroup_x(g):
+            regroup("x", g, x_raw[g])
 
-        def regroup_y(g):
-            t = stage.tile([P, PACK * W], BF16, tag="yg", name="yg", align_bytes=64)
-            nc.vector.tensor_copy(
-                out=t[:].rearrange("p (c f t) -> p c f t", c=GB, t=PACK),
-                in_=o1[g][:].rearrange("p c (t f) -> p c f t", t=PACK),
-            )
-            y_grouped[g] = t
+        def quantise_x(g):
+            quantise("x", g, keep, "%d" % g)
 
-        def quant_y(g):
-            y_codes[g] = stage.tile([P, W], U32, tag="yc", name="yc", align_bytes=64)
-            y_scales[g] = stage.tile([P, W], U8, tag="ys", name="ys", align_bytes=64)
-            nc.vector.quantize_mx(out=y_codes[g][:].bitcast(FP8X4), scales=y_scales[g][:], in_=y_grouped[g][:])
+        def first_hop(g):
+            x1_result[g] = hop("x", g, out_0)
 
-        def hop2(g):
-            o2[g] = outs.tile([P, GB, PACK * F], F32, tag="o", name="o2")
-            hop(y_codes[g], y_scales[g], o2[g], dram_group(out_1, g))
+        def regroup_x1(g):
+            regroup("x1", g, x1_result[g])
+
+        def quantise_x1(g):
+            quantise("x1", g, stage, "")
+
+        def second_hop(g):
+            x2_result[g] = hop("x1", g, out_1)
 
         def recurrence(g):
-            o3 = outs.tile([P, GB, PACK * F], F32, tag="o", name="o3")
+            xt2_result = results.tile([P, GROUP, ROW], F32, tag="result", name="xt2_result")
             nc.vector.scalar_tensor_tensor(
-                out=o3[:].rearrange("p c n -> p (c n)"),
-                in0=o2[g][:].rearrange("p c n -> p (c n)"),
+                out=xt2_result[:].rearrange("p c n -> p (c n)"),
+                in0=x2_result[g][:].rearrange("p c n -> p (c n)"),
                 scalar=2.0,
                 in1=x_raw[g][:].rearrange("p c n -> p (c n)"),
-                op0=MULT,
-                op1=SUB,
+                op0=mybir.AluOpType.mult,
+                op1=mybir.AluOpType.subtract,
             )
-            nc.sync.dma_start(out=dram_group(out_2, g), in_=o3[:])
+            nc.sync.dma_start(out=dram_group(out_2, g), in_=xt2_result[:])
 
         regroup_x(0)
-        quant_x(0)
-        quant_l()
-        hop1(0)
-        for g in (1, 2):
+        quantise_x(0)
+        quantise_l()
+        first_hop(0)
+        for g in range(1, AHEAD):
             regroup_x(g)
-            quant_x(g)
-            hop1(g)
-        for g in range(NG):
-            a = g + 3
-            regroup_y(g)
-            if a < NG:
+            quantise_x(g)
+            first_hop(g)
+        for g in range(N_GROUPS):
+            a = g + AHEAD
+            regroup_x1(g)
+            if a < N_GROUPS:
                 regroup_x(a)
-            quant_y(g)
-            hop2(g)
-            if a < NG:
-                quant_x(a)
-                hop1(a)
+            quantise_x1(g)
+            second_hop(g)
+            if a < N_GROUPS:
+                quantise_x(a)
+                first_hop(a)
             if g >= 1:
                 recurrence(g - 1)
-        recurrence(NG - 1)
+        recurrence(N_GROUPS - 1)

@@ -34,11 +34,11 @@ def tile_gcncheb_pa_t_kernel(tc, x, L, out_0, out_1, out_2):
         def dram_group(tensor, g):
             return tensor[g * GROUP:(g + 1) * GROUP].rearrange("c (p t) f -> p c (t f)", t=PACK)
 
-        l_raw = keep.tile([P, PACK * NODES], BF16, name="l_raw")
+        l_raw = keep.tile([P, PACK * NODES], BF16, name="l_raw", align_bytes=256)
         nc.sync.dma_start(out=l_raw[:], in_=L.rearrange("(q j) m -> q (j m)", j=PACK))
         x_raw = []
         for g in range(N_GROUPS):
-            x_raw.append(keep.tile([P, GROUP, ROW], BF16, name="x_raw%d" % g))
+            x_raw.append(keep.tile([P, GROUP, ROW], BF16, name="x_raw%d" % g, align_bytes=256))
             nc.sync.dma_start(out=x_raw[g][:], in_=dram_group(x, g))
 
         identity = keep.tile([P, P], F32, name="identity")
@@ -85,7 +85,7 @@ def tile_gcncheb_pa_t_kernel(tc, x, L, out_0, out_1, out_2):
             )
 
         def hop(name, g, destination):
-            result = results.tile([P, GROUP, ROW], F32, tag="result", name="result")
+            result = results.tile([P, GROUP, ROW], F32, tag="result", name="result", align_bytes=256)
             for j in range(PACK):
                 bank = psum.tile([P, GROUP, FEATURES], F32, tag="bank", name="bank")
                 nc.tensor.matmul_mx(
@@ -120,7 +120,7 @@ def tile_gcncheb_pa_t_kernel(tc, x, L, out_0, out_1, out_2):
             x2_result[g] = hop("x1", g, out_1)
 
         def recurrence(g):
-            xt2_result = results.tile([P, GROUP, ROW], F32, tag="result", name="xt2_result")
+            xt2_result = results.tile([P, GROUP, ROW], F32, tag="result", name="xt2_result", align_bytes=256)
             nc.vector.scalar_tensor_tensor(
                 out=xt2_result[:].rearrange("p c n -> p (c n)"),
                 in0=x2_result[g][:].rearrange("p c n -> p (c n)"),

@@ -34,11 +34,11 @@ def tile_gcncheb_pa_t_kernel(tc, x, L, out_0, out_1, out_2):
         def dram_group(tensor, g):
             return tensor[g * GROUP:(g + 1) * GROUP].rearrange("c (p t) f -> p c (t f)", t=PACK)
 
-        l_raw = keep.tile([P, PACK * NODES], BF16, name="l_raw", align_bytes=256)
+        l_raw = keep.tile([P, PACK * NODES], BF16, name="l_raw", align_bytes=4096)
         nc.sync.dma_start(out=l_raw[:], in_=L.rearrange("(q j) m -> q (j m)", j=PACK))
         x_raw = []
         for g in range(N_GROUPS):
-            x_raw.append(keep.tile([P, GROUP, ROW], BF16, name="x_raw%d" % g, align_bytes=256))
+            x_raw.append(keep.tile([P, GROUP, ROW], BF16, name="x_raw%d" % g, align_bytes=1024))
             nc.sync.dma_start(out=x_raw[g][:], in_=dram_group(x, g))
 
         identity = keep.tile([P, P], F32, name="identity")
@@ -85,7 +85,7 @@ def tile_gcncheb_pa_t_kernel(tc, x, L, out_0, out_1, out_2):
             )
 
         def hop(name, g, destination):
-            result = results.tile([P, GROUP, ROW], F32, tag="result", name="result", align_bytes=256)
+            result = results.tile([P, GROUP, ROW], F32, tag="result", name="result", align_bytes=2048)
             for j in range(PACK):
                 bank = psum.tile([P, GROUP, FEATURES], F32, tag="bank", name="bank")
                 nc.tensor.matmul_mx(
@@ -120,7 +120,7 @@ def tile_gcncheb_pa_t_kernel(tc, x, L, out_0, out_1, out_2):
             x2_result[g] = hop("x1", g, out_1)
 
         def recurrence(g):
-            xt2_result = results.tile([P, GROUP, ROW], F32, tag="result", name="xt2_result", align_bytes=256)
+            xt2_result = results.tile([P, GROUP, ROW], F32, tag="result", name="xt2_result", align_bytes=2048)
             nc.vector.scalar_tensor_tensor(
                 out=xt2_result[:].rearrange("p c n -> p (c n)"),
                 in0=x2_result[g][:].rearrange("p c n -> p (c n)"),
@@ -145,10 +145,11 @@ def tile_gcncheb_pa_t_kernel(tc, x, L, out_0, out_1, out_2):
             if a < N_GROUPS:
                 regroup_x(a)
             quantise_x1(g)
-            second_hop(g)
             if a < N_GROUPS:
                 quantise_x(a)
-                first_hop(a)
             if g >= 1:
                 recurrence(g - 1)
+            second_hop(g)
+            if a < N_GROUPS:
+                first_hop(a)
         recurrence(N_GROUPS - 1)

@@ -14,10 +14,12 @@ PACK = 4
 PAIRS = 2
 SETS_IN_BANK = 2
 BATCH, NODES, FEATURES = 32, 512, 128
-GROUP = 4
-N_GROUPS = BATCH // GROUP
-COLUMNS = GROUP * FEATURES
+GROUP_SIZES = (2, 2) + (4,) * 7
+N_GROUPS = len(GROUP_SIZES)
+FIRST_ITEM = [sum(GROUP_SIZES[:g]) for g in range(N_GROUPS)]
+assert sum(GROUP_SIZES) == BATCH
 ROW = PACK * FEATURES
+DMA_ALIGN = 256
 AHEAD = 3
 FLOPS = 2 * 2 * BATCH * NODES * NODES * FEATURES
 
@@ -32,25 +34,29 @@ def tile_gcncheb_pa_t_kernel(tc, x, L, out_0, out_1, out_2):
         ctx.enter_context(tc.manual_schedule())
 
         def dram_group(tensor, g):
-            return tensor[g * GROUP:(g + 1) * GROUP].rearrange("c (p t) f -> p c (t f)", t=PACK)
+            items = tensor[FIRST_ITEM[g]:FIRST_ITEM[g] + GROUP_SIZES[g]]
+            return items.rearrange("c (p t) f -> p c (t f)", t=PACK)
 
-        l_raw = keep.tile([P, PACK * NODES], BF16, name="l_raw", align_bytes=4096)
-        nc.sync.dma_start(out=l_raw[:], in_=L.rearrange("(q j) m -> q (j m)", j=PACK))
+        l_rows = L.rearrange("(q j) m -> q j m", j=PACK)
+        l_raw = []
+        for first_set in range(0, PACK, SETS_IN_BANK):
+            l_raw.append(keep.tile([P, SETS_IN_BANK, NODES], BF16, name="l_raw%d" % first_set, align_bytes=DMA_ALIGN))
+            nc.sync.dma_start(out=l_raw[-1][:], in_=l_rows[:, first_set:first_set + SETS_IN_BANK, :])
         x_raw = []
         for g in range(N_GROUPS):
-            x_raw.append(keep.tile([P, GROUP, ROW], BF16, name="x_raw%d" % g, align_bytes=1024))
+            x_raw.append(keep.tile([P, GROUP_SIZES[g], ROW], BF16, name="x_raw%d" % g, align_bytes=DMA_ALIGN))
             nc.sync.dma_start(out=x_raw[g][:], in_=dram_group(x, g))
 
         identity = keep.tile([P, P], F32, name="identity")
         masks.make_identity(nc, identity[:])
-        l_words = l_raw[:].bitcast(F32).rearrange("q (j p u) -> q j u p", j=PACK, u=PAIRS)
         l_grouped = keep.tile([P, PACK * NODES], BF16, name="l_grouped", align_bytes=64)
         l_grouped_words = l_grouped[:].bitcast(F32).rearrange("p (j q u) -> p j q u", j=PACK, u=PAIRS)
-        for first_set in range(0, PACK, SETS_IN_BANK):
+        for half, first_set in enumerate(range(0, PACK, SETS_IN_BANK)):
+            l_words = l_raw[half][:].bitcast(F32).rearrange("q s (p u) -> q s u p", u=PAIRS)
             transposed = psum.tile([P, SETS_IN_BANK * PAIRS, P], F32, tag="bank", name="transposed")
             for s in range(SETS_IN_BANK):
                 for u in range(PAIRS):
-                    nc.tensor.transpose(transposed[:, PAIRS * s + u, :], l_words[:, first_set + s, u, :], identity[:])
+                    nc.tensor.transpose(transposed[:, PAIRS * s + u, :], l_words[:, s, u, :], identity[:])
             nc.scalar.copy(
                 out=l_grouped_words[:, first_set:first_set + SETS_IN_BANK, :, :],
                 in_=transposed[:].rearrange("p (s u) q -> p s q u", u=PAIRS),
@@ -69,25 +75,26 @@ def tile_gcncheb_pa_t_kernel(tc, x, L, out_0, out_1, out_2):
 
         def regroup(name, g, source):
             label = name + "_grouped"
-            grouped[name, g] = stage.tile([P, PACK * COLUMNS], BF16, tag=label, name=label, align_bytes=64)
+            grouped[name, g] = stage.tile([P, GROUP_SIZES[g] * ROW], BF16, tag=label, name=label, align_bytes=64)
             nc.vector.tensor_copy(
-                out=grouped[name, g][:].rearrange("p (c f t) -> p c f t", c=GROUP, t=PACK),
+                out=grouped[name, g][:].rearrange("p (c f t) -> p c f t", c=GROUP_SIZES[g], t=PACK),
                 in_=source[:].rearrange("p c (t f) -> p c f t", t=PACK),
             )
 
         def quantise(name, g, pool, suffix):
+            columns = GROUP_SIZES[g] * FEATURES
             label = name + "_codes" + suffix
-            codes[name, g] = pool.tile([P, COLUMNS], U32, tag=label, name=label, align_bytes=64)
+            codes[name, g] = pool.tile([P, columns], U32, tag=label, name=label, align_bytes=64)
             label = name + "_scales" + suffix
-            scales[name, g] = pool.tile([P, COLUMNS], U8, tag=label, name=label, align_bytes=64)
+            scales[name, g] = pool.tile([P, columns], U8, tag=label, name=label, align_bytes=64)
             nc.vector.quantize_mx(
                 out=codes[name, g][:].bitcast(FP8X4), scales=scales[name, g][:], in_=grouped[name, g][:]
             )
 
         def hop(name, g, destination):
-            result = results.tile([P, GROUP, ROW], F32, tag="result", name="result", align_bytes=2048)
+            result = results.tile([P, GROUP_SIZES[g], ROW], F32, tag="result", name="result", align_bytes=DMA_ALIGN)
             for j in range(PACK):
-                bank = psum.tile([P, GROUP, FEATURES], F32, tag="bank", name="bank")
+                bank = psum.tile([P, GROUP_SIZES[g], FEATURES], F32, tag="bank", name="bank")
                 nc.tensor.matmul_mx(
                     out=bank[:].rearrange("p c f -> p (c f)"),
                     lhsT=l_codes[:, j * P:(j + 1) * P].bitcast(FP8X4),
@@ -120,7 +127,9 @@ def tile_gcncheb_pa_t_kernel(tc, x, L, out_0, out_1, out_2):
             x2_result[g] = hop("x1", g, out_1)
 
         def recurrence(g):
-            xt2_result = results.tile([P, GROUP, ROW], F32, tag="result", name="xt2_result", align_bytes=2048)
+            xt2_result = results.tile(
+                [P, GROUP_SIZES[g], ROW], F32, tag="result", name="xt2_result", align_bytes=DMA_ALIGN
+            )
             nc.vector.scalar_tensor_tensor(
                 out=xt2_result[:].rearrange("p c n -> p (c n)"),
                 in0=x2_result[g][:].rearrange("p c n -> p (c n)"),
@@ -133,9 +142,12 @@ def tile_gcncheb_pa_t_kernel(tc, x, L, out_0, out_1, out_2):
 
         regroup_x(0)
         quantise_x(0)
+        regroup_x(1)
         quantise_l()
         first_hop(0)
-        for g in range(1, AHEAD):
+        quantise_x(1)
+        first_hop(1)
+        for g in range(2, AHEAD):
             regroup_x(g)
             quantise_x(g)
             first_hop(g)

@@ -39,9 +39,9 @@ def tile_gcncheb_pa_t_kernel(tc, x, L, out_0, out_1, out_2):
 
         l_rows = L.rearrange("(q j) m -> q j m", j=PACK)
         l_raw = []
-        for first_set in range(0, PACK, SETS_IN_BANK):
-            l_raw.append(keep.tile([P, SETS_IN_BANK, NODES], BF16, name="l_raw%d" % first_set, align_bytes=DMA_ALIGN))
-            nc.sync.dma_start(out=l_raw[-1][:], in_=l_rows[:, first_set:first_set + SETS_IN_BANK, :])
+        for j in range(PACK):
+            l_raw.append(keep.tile([P, NODES], BF16, name="l_raw%d" % j, align_bytes=DMA_ALIGN))
+            nc.sync.dma_start(out=l_raw[j][:], in_=l_rows[:, j, :])
         x_raw = []
         for g in range(N_GROUPS):
             x_raw.append(keep.tile([P, GROUP_SIZES[g], ROW], BF16, name="x_raw%d" % g, align_bytes=DMA_ALIGN))
@@ -51,12 +51,12 @@ def tile_gcncheb_pa_t_kernel(tc, x, L, out_0, out_1, out_2):
         masks.make_identity(nc, identity[:])
         l_grouped = keep.tile([P, PACK * NODES], BF16, name="l_grouped", align_bytes=64)
         l_grouped_words = l_grouped[:].bitcast(F32).rearrange("p (j q u) -> p j q u", j=PACK, u=PAIRS)
-        for half, first_set in enumerate(range(0, PACK, SETS_IN_BANK)):
-            l_words = l_raw[half][:].bitcast(F32).rearrange("q s (p u) -> q s u p", u=PAIRS)
+        for first_set in range(0, PACK, SETS_IN_BANK):
             transposed = psum.tile([P, SETS_IN_BANK * PAIRS, P], F32, tag="bank", name="transposed")
             for s in range(SETS_IN_BANK):
+                l_words = l_raw[first_set + s][:].bitcast(F32).rearrange("q (p u) -> q u p", u=PAIRS)
                 for u in range(PAIRS):
-                    nc.tensor.transpose(transposed[:, PAIRS * s + u, :], l_words[:, s, u, :], identity[:])
+                    nc.tensor.transpose(transposed[:, PAIRS * s + u, :], l_words[:, u, :], identity[:])
             nc.scalar.copy(
                 out=l_grouped_words[:, first_set:first_set + SETS_IN_BANK, :, :],
                 in_=transposed[:].rearrange("p (s u) q -> p s q u", u=PAIRS),

from contextlib import ExitStack

import concourse.masks as masks
import concourse.mybir as mybir

F32 = mybir.dt.float32
BF16 = mybir.dt.bfloat16
U32 = mybir.dt.uint32
U8 = mybir.dt.uint8
FP8X4 = mybir.dt.float8_e4m3fn_x4

P = 128
PACK = 4
PAIRS = 2
SETS_IN_BANK = 2
BATCH, NODES, FEATURES = 32, 512, 128
GROUP_SIZES = (2, 2) + (4,) * 7
N_GROUPS = len(GROUP_SIZES)
FIRST_ITEM = [sum(GROUP_SIZES[:g]) for g in range(N_GROUPS)]
assert sum(GROUP_SIZES) == BATCH
ROW = PACK * FEATURES
DMA_ALIGN = 256
AHEAD = 3
FLOPS = 2 * 2 * BATCH * NODES * NODES * FEATURES


def tile_gcncheb_pa_t_kernel(tc, x, L, out_0, out_1, out_2):
    nc = tc.nc
    with ExitStack() as ctx:
        keep = ctx.enter_context(tc.tile_pool(name="keep", bufs=1))
        stage = ctx.enter_context(tc.tile_pool(name="stage", bufs=3))
        results = ctx.enter_context(tc.tile_pool(name="results", bufs=16))
        psum = ctx.enter_context(tc.psum_pool(name="psum", bufs=8))
        ctx.enter_context(tc.manual_schedule())

        def dram_group(tensor, g):
            items = tensor[FIRST_ITEM[g]:FIRST_ITEM[g] + GROUP_SIZES[g]]
            return items.rearrange("c (p t) f -> p c (t f)", t=PACK)

        l_rows = L.rearrange("(q j) m -> q j m", j=PACK)
        l_raw = []
        for j in range(PACK):
            l_raw.append(keep.tile([P, NODES], BF16, name="l_raw%d" % j, align_bytes=DMA_ALIGN))
            nc.sync.dma_start(out=l_raw[j][:], in_=l_rows[:, j, :])
        x_raw = []
        for g in range(N_GROUPS):
            x_raw.append(keep.tile([P, GROUP_SIZES[g], ROW], BF16, name="x_raw%d" % g, align_bytes=DMA_ALIGN))
            nc.sync.dma_start(out=x_raw[g][:], in_=dram_group(x, g))

        identity = keep.tile([P, P], F32, name="identity")
        masks.make_identity(nc, identity[:])
        l_grouped = keep.tile([P, PACK * NODES], BF16, name="l_grouped", align_bytes=64)
        l_grouped_words = l_grouped[:].bitcast(F32).rearrange("p (j q u) -> p j q u", j=PACK, u=PAIRS)
        for first_set in range(0, PACK, SETS_IN_BANK):
            transposed = psum.tile([P, SETS_IN_BANK * PAIRS, P], F32, tag="bank", name="transposed")
            for s in range(SETS_IN_BANK):
                l_words = l_raw[first_set + s][:].bitcast(F32).rearrange("q (p u) -> q u p", u=PAIRS)
                for u in range(PAIRS):
                    nc.tensor.transpose(transposed[:, PAIRS * s + u, :], l_words[:, u, :], identity[:])
            nc.scalar.copy(
                out=l_grouped_words[:, first_set:first_set + SETS_IN_BANK, :, :],
                in_=transposed[:].rearrange("p (s u) q -> p s q u", u=PAIRS),
            )
        l_codes = keep.tile([P, NODES], U32, name="l_codes", align_bytes=64)
        l_scales = keep.tile([P, NODES], U8, name="l_scales", align_bytes=64)

        def quantise_l():
            nc.vector.quantize_mx(out=l_codes[:].bitcast(FP8X4), scales=l_scales[:], in_=l_grouped[:])

        grouped = {}
        codes = {}
        scales = {}
        x1_result = {}
        x2_result = {}

        def regroup(name, g, source):
            label = name + "_grouped"
            grouped[name, g] = stage.tile([P, GROUP_SIZES[g] * ROW], BF16, tag=label, name=label, align_bytes=64)
            nc.vector.tensor_copy(
                out=grouped[name, g][:].rearrange("p (c f t) -> p c f t", c=GROUP_SIZES[g], t=PACK),
                in_=source[:].rearrange("p c (t f) -> p c f t", t=PACK),
            )

        def quantise(name, g, pool, suffix):
            columns = GROUP_SIZES[g] * FEATURES
            label = name + "_codes" + suffix
            codes[name, g] = pool.tile([P, columns], U32, tag=label, name=label, align_bytes=64)
            label = name + "_scales" + suffix
            scales[name, g] = pool.tile([P, columns], U8, tag=label, name=label, align_bytes=64)
            nc.vector.quantize_mx(
                out=codes[name, g][:].bitcast(FP8X4), scales=scales[name, g][:], in_=grouped[name, g][:]
            )

        def hop(name, g, destination):
            result = results.tile([P, GROUP_SIZES[g], ROW], F32, tag="result", name="result", align_bytes=DMA_ALIGN)
            for j in range(PACK):
                bank = psum.tile([P, GROUP_SIZES[g], FEATURES], F32, tag="bank", name="bank")
                nc.tensor.matmul_mx(
                    out=bank[:].rearrange("p c f -> p (c f)"),
                    lhsT=l_codes[:, j * P:(j + 1) * P].bitcast(FP8X4),
                    lhsT_scale=l_scales[:, j * P:(j + 1) * P],
                    rhs=codes[name, g][:].bitcast(FP8X4),
                    rhs_scale=scales[name, g][:],
                    start=True,
                    stop=True,
                )
                nc.scalar.copy(out=result[:, :, j * FEATURES:(j + 1) * FEATURES], in_=bank[:])
            nc.sync.dma_start(out=dram_group(destination, g), in_=result[:])
            return result

        def regroup_x(g):
            regroup("x", g, x_raw[g])

        def quantise_x(g):
            quantise("x", g, keep, "%d" % g)

        def first_hop(g):
            x1_result[g] = hop("x", g, out_0)

        def regroup_x1(g):
            regroup("x1", g, x1_result[g])

        def quantise_x1(g):
            quantise("x1", g, stage, "")

        def second_hop(g):
            x2_result[g] = hop("x1", g, out_1)

        def recurrence(g):
            xt2_result = results.tile(
                [P, GROUP_SIZES[g], ROW], F32, tag="result", name="xt2_result", align_bytes=DMA_ALIGN
            )
            nc.vector.scalar_tensor_tensor(
                out=xt2_result[:].rearrange("p c n -> p (c n)"),
                in0=x2_result[g][:].rearrange("p c n -> p (c n)"),
                scalar=2.0,
                in1=x_raw[g][:].rearrange("p c n -> p (c n)"),
                op0=mybir.AluOpType.mult,
                op1=mybir.AluOpType.subtract,
            )
            nc.sync.dma_start(out=dram_group(out_2, g), in_=xt2_result[:])

        regroup_x(0)
        quantise_x(0)
        regroup_x(1)
        quantise_l()
        first_hop(0)
        quantise_x(1)
        first_hop(1)
        for g in range(2, AHEAD):
            regroup_x(g)
            quantise_x(g)
            first_hop(g)
        for g in range(N_GROUPS):
            a = g + AHEAD
            regroup_x1(g)
            if a < N_GROUPS:
                regroup_x(a)
            quantise_x1(g)
            if a < N_GROUPS:
                quantise_x(a)
            if g >= 1:
                recurrence(g - 1)
            second_hop(g)
            if a < N_GROUPS:
                first_hop(a)
        recurrence(N_GROUPS - 1)
